import numpy as np
import ml_dtypes


def mxq(x, axis, fmt="e4m3"):
    dtype, down = {"e4m3": (ml_dtypes.float8_e4m3fn, 7), "e5m2": (ml_dtypes.float8_e5m2, 14)}[fmt]
    v = np.moveaxis(np.asarray(x, np.float32).astype(ml_dtypes.bfloat16).astype(np.float64), axis, -1)
    blocks = v.reshape(v.shape[:-1] + (-1, 32))
    amax = np.abs(blocks).max(-1, keepdims=True)
    byte = np.maximum(np.where(amax > 0, np.frexp(amax)[1] - 1 + 127, 0) - down, 1)
    scale = np.exp2(byte - 127.0)
    codes = (blocks / scale).astype(np.float32).astype(dtype).astype(np.float64)
    return np.moveaxis((codes * scale).reshape(v.shape), -1, axis)


WIDE = False


def mx_kscale(k):
    if not WIDE:
        return np.ones(k)
    levels = np.array([18, -18])
    if k % 512:
        return np.exp2(np.random.permutation(np.resize(levels, k // 32))).repeat(32)
    a = np.empty((k // 512, 16))
    for p in range(k // 512):
        a[p, :8] = np.random.permutation(np.resize(levels, 8))
        for g in range(8):
            far = levels[np.abs(levels - a[p, g]) >= 10]
            a[p, g + 8] = far[np.random.randint(len(far))]
    return np.exp2(a.ravel()).repeat(32)


BF16 = ml_dtypes.bfloat16


def bf(x):
    return np.asarray(x, np.float32).astype(BF16)


def f64(x):
    return np.asarray(x).astype(np.float64)


B, N, C, R, CO, L = 2, 512, 512, 128, 512, 2
C3 = 3 * C
EPS = 1e-5
LOGIT_STD = 2.5
X_STD = 1.5


def setup_inputs():
    u = mx_kscale(CO)
    v = mx_kscale(N)
    s = mx_kscale(B * C).reshape(B, C)
    sc = s[0]
    sb = np.clip(s[:, 0] / s[0, 0], 2.0 ** -8, 2.0 ** 8)
    col = np.concatenate([np.ones(C), 1.0 / (sc * v.max()), 1.0 / sc])
    e = np.exp(np.maximum(np.random.standard_normal((N, N)) * LOGIT_STD, 0.0))
    h = bf(np.random.standard_normal((B, C, N)) * X_STD)
    x1_0 = bf(np.random.standard_normal((B, C, N)) * 0.4)
    adp_0 = bf(e / e.sum(1, keepdims=True))
    wg_0 = bf(np.random.standard_normal((CO, C3)) / np.sqrt(C))
    bg = bf(np.random.standard_normal(C) * 0.2)
    gamma = bf(1.0 + 0.1 * np.random.standard_normal(C))
    beta = bf(np.random.standard_normal(C) * 0.2)
    rmean = bf(np.random.standard_normal(C) * 0.2)
    rvar = bf(np.random.uniform(0.5, 1.5, C))
    rstd = 1.0 / np.sqrt(f64(rvar) + EPS)
    g = np.random.standard_normal((B, CO, N)) * np.exp2(np.random.randint(-6, 1, (B, 1, N)))
    g = bf(g * u[None, :, None] * v[None, None, :] / sb[:, None, None])
    return {"h": h,
            "x1": bf(f64(x1_0) * sb[:, None, None] * sc[None, :, None]),
            "adp": bf(f64(adp_0) / v[:, None]),
            "wg": bf(f64(wg_0) / u[:, None] * col[None, :]),
            "bg": bg,
            "gamma": gamma,
            "beta": beta,
            "rmean": rmean,
            "rvar": rvar,
            "rstd": np.asarray(rstd, np.float32),
            "grad_out": g}


def reference(h, x1, adp, wg, bg, gamma, beta, rmean, rvar, rstd, grad_out):
    dz2 = f64(grad_out) * (f64(gamma) * f64(rstd))[None, :, None]
    w = mxq(f64(wg)[:, C:], 0, "e4m3")
    d = w.T @ mxq(dz2, 1, "e5m2")
    d1 = d[:, :C]
    d2 = d[:, C:].reshape(B * C, N)
    hop = mxq(d2, 1, "e5m2") @ mxq(f64(adp), 0, "e4m3")
    dx1 = hop.reshape(B, C, N) + d1
    x1r = f64(x1).reshape(B * C, N)
    dadp = mxq(d2, 0, "e5m2").T @ mxq(x1r, 0, "e4m3")
    return dx1, dadp

@@ -1,0 +1,332 @@
+from contextlib import ExitStack
+
+import concourse.mybir as mybir
+from concourse.masks import make_identity
+
+FLOPS = 2 * (2 * 512 * 1024 * 512) + 2 * 1024 * 512 * 512 + 2 * 512 * 1024 * 512
+BYTES = 2 * (2 * 512 * 512 + 512 * 1024 + 2 * 512 * 512 + 512 * 512 + 512) + 4 * 512 + 4 * (2 * 512 * 512 + 512 * 512)
+
+F32 = mybir.dt.float32
+BF16 = mybir.dt.bfloat16
+U32 = mybir.dt.uint32
+U8 = mybir.dt.uint8
+E4M3 = mybir.dt.float8_e4m3fn_x4
+E5M2 = mybir.dt.float8_e5m2_x4
+MULT = mybir.AluOpType.mult
+
+P = 128
+N = 512
+B = 2
+
+
+def tile_spatialgcn_pb_v_kernel(
+    tc, h, x1, adp, wg, bg, gamma, beta, rmean, rvar, rstd, grad_out, out_0, out_1
+):
+    nc = tc.nc
+    with ExitStack() as ctx:
+        sb = ctx.enter_context(tc.tile_pool(name="sb", bufs=1))
+        ps = ctx.enter_context(tc.psum_pool(name="ps", bufs=1))
+
+        def tile(name, shape, dtype):
+            return sb.tile([P] + shape, dtype, name=name, align_bytes=256)
+
+        gam = tile("gam", [4], BF16)
+        rst = tile("rst", [4], F32)
+        fac = tile("fac", [4], F32)
+        ident = tile("ident", [P], F32)
+        identb = tile("identb", [P], BF16)
+        graw = [tile("graw%d" % b, [4, N], BF16) for b in range(B)]
+        dz = [tile("dz%d" % b, [4, N], BF16) for b in range(B)]
+        dzi = [tile("dzi%d" % b, [N, 4], BF16) for b in range(B)]
+        dzq = [tile("dzq%d" % b, [N], U32) for b in range(B)]
+        dzs = [tile("dzs%d" % b, [N], U8) for b in range(B)]
+        wraw = [tile("wraw%d" % k, [4, N], BF16) for k in range(2)]
+        wi = [tile("wi%d" % k, [4, P, 4], BF16) for k in range(2)]
+        wq = [tile("wq%d" % k, [N], U32) for k in range(2)]
+        ws = [tile("ws%d" % k, [N], U8) for k in range(2)]
+        xraw = [tile("xraw%d" % b, [4, N], BF16) for b in range(B)]
+        xi = [tile("xi%d" % b, [N, 4], BF16) for b in range(B)]
+        xq = [tile("xq%d" % b, [N], U32) for b in range(B)]
+        xs = [tile("xs%d" % b, [N], U8) for b in range(B)]
+        araw = tile("araw", [4, N], BF16)
+        ai = tile("ai", [N, 4], BF16)
+        aq = tile("aq", [N], U32)
+        asc = tile("asc", [N], U8)
+        ev = [tile("ev%d" % b, [4, N], BF16) for b in range(B)]
+        di = [tile("di%d" % b, [N, 4], BF16) for b in range(B)]
+        dq = [tile("dq%d" % b, [N], U32) for b in range(B)]
+        ds = [tile("ds%d" % b, [N], U8) for b in range(B)]
+        ti = [tile("ti%d" % b, [4, P, 4], BF16) for b in range(B)]
+        tq = [tile("tq%d" % b, [N], U32) for b in range(B)]
+        ts = [tile("ts%d" % b, [N], U8) for b in range(B)]
+        o0 = [tile("o0_%d" % b, [4, N], F32) for b in range(B)]
+        o1 = tile("o1", [4, N], F32)
+
+        V, S = nc.vector, nc.scalar
+        nbank = [0]
+        bank = {}
+
+        def alloc(key, shape=(N,), dtype=F32):
+            k = nbank[0] % 8
+            nbank[0] += 1
+            bank[key] = ps.tile([P] + list(shape), dtype, name="pb%d" % k, tag="pb%d" % k)
+            return bank[key]
+
+        def cp(eng, out, in_):
+            if eng is nc.scalar:
+                eng.copy(out=out, in_=in_)
+            else:
+                eng.tensor_copy(out=out, in_=in_)
+
+        def scale(b, j):
+            V.tensor_scalar(out=dz[b][:, j, :], in0=graw[b][:, j, :], scalar1=fac[:, j : j + 1], scalar2=None, op0=MULT)
+
+        def cols(lo, hi):
+            return slice(lo * N // 8, hi * N // 8)
+
+        def il(eng, dst, src, lo, hi):
+            c = cols(lo, hi)
+            cp(eng, dst[:, c, :], src[:, :, c].rearrange("p t n -> p n t"))
+
+        def il_w(eng, k, t0, t1):
+            cp(eng, wi[k][:, t0:t1], wraw[k][:].rearrange("p j (m t) -> p t m j", t=4)[:, t0:t1])
+
+        def mv(key, views):
+            x = alloc(("m", key), (2 * N,), BF16)
+            at = 0
+            for v in views:
+                n = 4 * v.shape[1]
+                nc.tensor.matmul(
+                    out=x[:, at : at + n].rearrange("p (n t) -> p n t", t=4), lhsT=identb[:], rhs=v, start=True, stop=True
+                )
+                at += n
+
+        def mv_il(key, src, lo, hi):
+            c = cols(lo, hi)
+            v = src[:].rearrange("p t n -> p n t")
+            mv(key, [v[:, a : min(a + P, c.stop), :] for a in range(c.start, c.stop, P)])
+
+        def mv_w(key, k, t0, t1):
+            v = wraw[k][:].rearrange("p j (m t) -> p t m j", t=4)
+            mv(key, [v[:, t] for t in range(t0, t1)])
+
+        def mc(eng, key, dst, lo, hi):
+            c = cols(lo, hi)
+            cp(eng, dst.rearrange("p n t -> p (n t)")[:, 4 * c.start : 4 * c.stop], bank["m", key][:, : 4 * (c.stop - c.start)])
+
+        def quant(codes, scales, src, lo, hi, fmt):
+            c = cols(lo, hi)
+            V.quantize_mx(
+                out=codes[:, c].bitcast(fmt),
+                scales=scales[:, c],
+                in_=src.rearrange("p n t -> p (n t)")[:, 4 * c.start : 4 * c.stop],
+            )
+
+        def q_dz(b, lo, hi):
+            quant(dzq[b], dzs[b], dzi[b][:], lo, hi, E5M2)
+
+        def q_w(k, t0, t1):
+            quant(wq[k], ws[k], wi[k][:].rearrange("p t m j -> p (t m) j"), 2 * t0, 2 * t1, E4M3)
+
+        def q_x(b, lo, hi):
+            quant(xq[b], xs[b], xi[b][:], lo, hi, E4M3)
+
+        def q_a(lo, hi):
+            quant(aq, asc, ai[:], lo, hi, E4M3)
+
+        def q_d(b, lo, hi):
+            quant(dq[b], ds[b], di[b][:], lo, hi, E5M2)
+
+        def q_t(b, t0, t1):
+            quant(tq[b], ts[b], ti[b][:].rearrange("p t c e -> p (t c) e"), 2 * t0, 2 * t1, E5M2)
+
+        def mx(out, l, ls, lf, i, r, rs, rf, start, stop):
+            m = slice(P * i, P * i + P)
+            nc.tensor.matmul_mx(
+                out=out[:],
+                lhsT=l[:, m].bitcast(lf),
+                lhsT_scale=ls[:, m],
+                rhs=r[:].bitcast(rf),
+                rhs_scale=rs[:],
+                start=start,
+                stop=stop,
+            )
+
+        def d2(b, t):
+            mx(alloc(("d", b, t)), wq[1], ws[1], E4M3, t, dzq[b], dzs[b], E5M2, True, True)
+
+        def evd(eng, b, t):
+            cp(eng, ev[b][:, t, :], bank["d", b, t][:])
+
+        def tr(b, t0):
+            x = alloc(("x", b, t0), (2, 2, P))
+            for t in range(2):
+                w = ev[b][:, t0 + t, :].bitcast(F32)
+                for u in range(2):
+                    nc.tensor.transpose(x[:, t, u, :], w[:, u::2], ident[:])
+
+        def wc(eng, b, t0):
+            cp(
+                eng,
+                ti[b][:, t0 : t0 + 2].rearrange("p t c e -> p t (c e)").bitcast(F32).rearrange("p t (c u) -> p t c u", u=2),
+                bank["x", b, t0][:].rearrange("p t u c -> p t c u"),
+            )
+
+        def d1(b, t):
+            mx(alloc(("o", b, t)), wq[0], ws[0], E4M3, t, dzq[b], dzs[b], E5M2, True, False)
+
+        def hop(b, t):
+            mx(bank["o", b, t], tq[b], ts[b], E5M2, t, aq, asc, E4M3, False, True)
+
+        def dadp(b, i):
+            if b == 0:
+                alloc(("a", i))
+            mx(bank["a", i], dq[b], ds[b], E5M2, i, xq[b], xs[b], E4M3, b == 0, b == B - 1)
+
+        def evo(eng, b, t):
+            cp(eng, o0[b][:, t, :], bank["o", b, t][:])
+
+        def eva(eng, i):
+            cp(eng, o1[:, i, :], bank["a", i][:])
+
+        def st_o(b, t0, t1):
+            nc.sync.dma_start(out=out_0[b].rearrange("(p t) v -> p t v", t=4)[:, t0:t1, :], in_=o0[b][:, t0:t1, :])
+
+        def st_a(i):
+            nc.sync.dma_start(out=out_1[P * i : P * i + P, :], in_=o1[:, i, :])
+
+        def ld(dst, src):
+            nc.sync.dma_start(out=dst, in_=src)
+
+        pj = "(p j) n -> p j n"
+        with tc.manual_schedule():
+            nc.scalar.dma_start(out=gam[:], in_=gamma.rearrange("(p j) -> p j", j=4))
+            nc.scalar.dma_start(out=rst[:], in_=rstd.rearrange("(p j) -> p j", j=4))
+            make_identity(nc, identb[:])
+            make_identity(nc, ident[:])
+            for j in (0, 2):
+                ld(graw[0][:, j : j + 2, :], grad_out[0].rearrange(pj, j=4)[:, j : j + 2, :])
+            ld(wraw[1][:], wg[:, 1024:1536].rearrange(pj, j=4))
+            ld(graw[1][:], grad_out[1].rearrange(pj, j=4))
+            ld(araw[:], adp.rearrange(pj, j=4))
+            ld(wraw[0][:], wg[:, 512:1024].rearrange(pj, j=4))
+            for b in range(B):
+                ld(xraw[b][:], x1[b].rearrange(pj, j=4))
+            V.tensor_tensor(out=fac[:], in0=gam[:], in1=rst[:], op=MULT)
+            scale(0, 0)
+            scale(0, 1)
+            scale(0, 2)
+            scale(0, 3)
+            mv_il("z01", dz[0], 5, 8)
+            il_w(V, 1, 0, 2)
+            q_w(1, 0, 2)
+            il(S, dzi[0], dz[0], 0, 5)
+            mv_w("w21", 1, 2, 4)
+            mc(S, "z01", dzi[0][:], 5, 8)
+            scale(1, 0)
+            scale(1, 1)
+            mv_il("a0", araw, 0, 4)
+            mc(S, "w21", wi[1][:].rearrange("p t m j -> p (t m) j"), 4, 8)
+            q_dz(0, 0, 8)
+            mc(S, "a0", ai[:], 0, 4)
+            scale(1, 2)
+            scale(1, 3)
+            q_w(1, 2, 4)
+            d2(0, 0)
+            d2(0, 1)
+            d2(0, 2)
+            evd(S, 0, 0)
+            evd(S, 0, 1)
+            d2(0, 3)
+            il(V, dzi[1], dz[1], 0, 4)
+            il(V, dzi[1], dz[1], 4, 8)
+            evd(S, 0, 2)
+            mv_il("a1", araw, 4, 8)
+            tr(0, 0)
+            il_w(V, 0, 0, 2)
+            evd(S, 0, 3)
+            q_dz(1, 0, 8)
+            wc(S, 0, 0)
+            q_w(0, 0, 2)
+            mc(S, "a1", ai[:], 4, 8)
+            il(V, xi[0], xraw[0], 0, 4)
+            q_t(0, 0, 2)
+            mv_il("x10", xraw[1], 0, 4)
+            mc(S, "x10", xi[1][:], 0, 4)
+            d2(1, 0)
+            d2(1, 1)
+            q_a(0, 8)
+            tr(0, 2)
+            il_w(V, 0, 2, 4)
+            d2(1, 2)
+            d1(0, 0)
+            hop(0, 0)
+            d2(1, 3)
+            wc(V, 0, 2)
+            il(V, xi[0], xraw[0], 4, 8)
+            evd(S, 1, 0)
+            d1(0, 1)
+            hop(0, 1)
+            il(V, di[0], ev[0], 0, 4)
+            evd(S, 1, 1)
+            q_w(0, 2, 4)
+            q_t(0, 2, 4)
+            evd(S, 1, 2)
+            evo(S, 0, 0)
+            q_d(0, 0, 4)
+            tr(1, 0)
+            evd(S, 1, 3)
+            tr(1, 2)
+            evo(S, 0, 1)
+            mv_il("d10", ev[1], 0, 4)
+            d1(0, 2)
+            hop(0, 2)
+            wc(S, 1, 0)
+            wc(S, 1, 2)
+            d1(0, 3)
+            hop(0, 3)
+            mc(S, "d10", di[1][:], 0, 4)
+            q_t(1, 0, 2)
+            d1(1, 0)
+            hop(1, 0)
+            q_x(0, 0, 8)
+            il(V, xi[1], xraw[1], 4, 8)
+            q_t(1, 2, 4)
+            q_x(1, 0, 8)
+            q_d(1, 0, 4)
+            il(V, di[0], ev[0], 4, 8)
+            st_o(0, 0, 2)
+            d1(1, 1)
+            hop(1, 1)
+            d1(1, 2)
+            hop(1, 2)
+            il(V, di[1], ev[1], 4, 8)
+            evo(S, 0, 2)
+            q_d(0, 4, 8)
+            evo(S, 0, 3)
+            dadp(0, 0)
+            dadp(1, 0)
+            evo(S, 1, 0)
+            evo(S, 1, 1)
+            evo(S, 1, 2)
+            eva(S, 0)
+            d1(1, 3)
+            hop(1, 3)
+            st_o(0, 2, 4)
+            dadp(0, 1)
+            evo(S, 1, 3)
+            dadp(1, 1)
+            st_o(1, 0, 2)
+            st_a(0)
+            dadp(0, 2)
+            st_o(1, 2, 4)
+            q_d(1, 4, 8)
+            dadp(1, 2)
+            dadp(0, 3)
+            eva(S, 1)
+            eva(S, 2)
+            dadp(1, 3)
+            eva(S, 3)
+            st_a(1)
+            st_a(2)
+            st_a(3)

@@ -86,7 +86,7 @@ def tile_spatialgcn_pb_v_kernel(
 
         def il(eng, dst, src, lo, hi):
             c = cols(lo, hi)
-            cp(eng, dst[:, c, :], src[:, :, c].rearrange("p t n -> p n t"))
+            cp(eng, dst[:, c, :].rearrange("p (n i) t -> p n t i", i=4), src[:, :, c].rearrange("p t (n i) -> p n t i", i=4))
 
         def il_w(eng, k, t0, t1):
             cp(eng, wi[k][:, t0:t1], wraw[k][:].rearrange("p j (m t) -> p t m j", t=4)[:, t0:t1])
@@ -217,116 +217,110 @@ def tile_spatialgcn_pb_v_kernel(
             scale(0, 1)
             scale(0, 2)
             scale(0, 3)
-            mv_il("z01", dz[0], 5, 8)
+            il(V, dzi[0], dz[0], 0, 5)
             il_w(V, 1, 0, 2)
-            q_w(1, 0, 2)
-            il(S, dzi[0], dz[0], 0, 5)
-            mv_w("w21", 1, 2, 4)
-            mc(S, "z01", dzi[0][:], 5, 8)
             scale(1, 0)
             scale(1, 1)
-            mv_il("a0", araw, 0, 4)
-            mc(S, "w21", wi[1][:].rearrange("p t m j -> p (t m) j"), 4, 8)
-            q_dz(0, 0, 8)
-            mc(S, "a0", ai[:], 0, 4)
+            il(S, dzi[0], dz[0], 5, 8)
+            q_w(1, 0, 2)
             scale(1, 2)
             scale(1, 3)
+            q_dz(0, 0, 8)
+            il_w(S, 1, 2, 4)
             q_w(1, 2, 4)
+            il(S, ai, araw, 0, 4)
             d2(0, 0)
+            il(S, dzi[1], dz[1], 0, 4)
+            il(V, dzi[1], dz[1], 4, 8)
+            il(V, ai, araw, 4, 8)
+            q_dz(1, 0, 8)
             d2(0, 1)
-            d2(0, 2)
             evd(S, 0, 0)
             evd(S, 0, 1)
-            d2(0, 3)
-            il(V, dzi[1], dz[1], 0, 4)
-            il(V, dzi[1], dz[1], 4, 8)
+            il(V, xi[0], xraw[0], 0, 4)
+            d2(0, 2)
+            d2(1, 0)
             evd(S, 0, 2)
-            mv_il("a1", araw, 4, 8)
+            evd(S, 1, 0)
+            d2(1, 1)
             tr(0, 0)
             il_w(V, 0, 0, 2)
-            evd(S, 0, 3)
-            q_dz(1, 0, 8)
-            wc(S, 0, 0)
-            q_w(0, 0, 2)
-            mc(S, "a1", ai[:], 4, 8)
-            il(V, xi[0], xraw[0], 0, 4)
-            q_t(0, 0, 2)
-            mv_il("x10", xraw[1], 0, 4)
-            mc(S, "x10", xi[1][:], 0, 4)
-            d2(1, 0)
-            d2(1, 1)
-            q_a(0, 8)
-            tr(0, 2)
-            il_w(V, 0, 2, 4)
+            evd(S, 1, 1)
+            d2(0, 3)
             d2(1, 2)
+            il_w(V, 0, 2, 4)
+            d2(1, 3)
+            q_a(0, 8)
+            wc(S, 0, 0)
+            q_t(0, 0, 2)
+            q_w(0, 0, 2)
+            evd(S, 0, 3)
+            evd(V, 1, 2)
+            il(V, xi[1], xraw[1], 0, 4)
+            tr(1, 0)
+            tr(0, 2)
+            evd(S, 1, 3)
+            wc(S, 1, 0)
+            wc(S, 0, 2)
             d1(0, 0)
             hop(0, 0)
-            d2(1, 3)
-            wc(V, 0, 2)
-            il(V, xi[0], xraw[0], 4, 8)
-            evd(S, 1, 0)
+            evo(S, 0, 0)
             d1(0, 1)
             hop(0, 1)
-            il(V, di[0], ev[0], 0, 4)
-            evd(S, 1, 1)
-            q_w(0, 2, 4)
-            q_t(0, 2, 4)
-            evd(S, 1, 2)
-            evo(S, 0, 0)
-            q_d(0, 0, 4)
-            tr(1, 0)
-            evd(S, 1, 3)
             tr(1, 2)
             evo(S, 0, 1)
-            mv_il("d10", ev[1], 0, 4)
-            d1(0, 2)
-            hop(0, 2)
-            wc(S, 1, 0)
-            wc(S, 1, 2)
-            d1(0, 3)
-            hop(0, 3)
-            mc(S, "d10", di[1][:], 0, 4)
             q_t(1, 0, 2)
+            wc(S, 1, 2)
+            q_t(0, 2, 4)
             d1(1, 0)
             hop(1, 0)
-            q_x(0, 0, 8)
-            il(V, xi[1], xraw[1], 4, 8)
-            q_t(1, 2, 4)
-            q_x(1, 0, 8)
-            q_d(1, 0, 4)
-            il(V, di[0], ev[0], 4, 8)
+            il(V, di[0], ev[0], 0, 4)
+            q_w(0, 2, 4)
+            il(V, di[1], ev[1], 0, 4)
+            evo(S, 1, 0)
             st_o(0, 0, 2)
+            il(V, xi[1], xraw[1], 4, 8)
+            q_d(0, 0, 4)
             d1(1, 1)
             hop(1, 1)
+            d1(0, 2)
+            hop(0, 2)
+            evo(S, 1, 1)
+            il(S, xi[0], xraw[0], 4, 8)
+            st_o(1, 0, 2)
+            q_t(1, 2, 4)
+            d1(0, 3)
+            hop(0, 3)
+            q_d(1, 0, 4)
+            evo(S, 0, 2)
             d1(1, 2)
             hop(1, 2)
-            il(V, di[1], ev[1], 4, 8)
-            evo(S, 0, 2)
-            q_d(0, 4, 8)
+            q_x(1, 0, 8)
             evo(S, 0, 3)
-            dadp(0, 0)
-            dadp(1, 0)
-            evo(S, 1, 0)
-            evo(S, 1, 1)
-            evo(S, 1, 2)
-            eva(S, 0)
+            q_x(0, 0, 8)
             d1(1, 3)
             hop(1, 3)
-            st_o(0, 2, 4)
+            dadp(0, 0)
             dadp(0, 1)
-            evo(S, 1, 3)
+            dadp(1, 0)
+            st_o(0, 2, 4)
+            il(V, di[0], ev[0], 4, 8)
+            il(V, di[1], ev[1], 4, 8)
+            q_d(0, 4, 8)
+            evo(S, 1, 2)
             dadp(1, 1)
-            st_o(1, 0, 2)
-            st_a(0)
-            dadp(0, 2)
-            st_o(1, 2, 4)
+            evo(S, 1, 3)
             q_d(1, 4, 8)
+            st_o(1, 2, 4)
+            dadp(0, 2)
+            eva(S, 0)
+            st_a(0)
             dadp(1, 2)
-            dadp(0, 3)
             eva(S, 1)
+            st_a(1)
+            dadp(0, 3)
             eva(S, 2)
+            st_a(2)
             dadp(1, 3)
             eva(S, 3)
-            st_a(1)
-            st_a(2)
             st_a(3)

@@ -34,7 +34,6 @@ def tile_spatialgcn_pb_v_kernel(
         rst = tile("rst", [4], F32)
         fac = tile("fac", [4], F32)
         ident = tile("ident", [P], F32)
-        identb = tile("identb", [P], BF16)
         graw = [tile("graw%d" % b, [4, N], BF16) for b in range(B)]
         dz = [tile("dz%d" % b, [4, N], BF16) for b in range(B)]
         dzi = [tile("dzi%d" % b, [N, 4], BF16) for b in range(B)]
@@ -90,29 +89,6 @@ def tile_spatialgcn_pb_v_kernel(
 
         def il_w(eng, k, t0, t1):
             cp(eng, wi[k][:, t0:t1], wraw[k][:].rearrange("p j (m t) -> p t m j", t=4)[:, t0:t1])
-
-        def mv(key, views):
-            x = alloc(("m", key), (2 * N,), BF16)
-            at = 0
-            for v in views:
-                n = 4 * v.shape[1]
-                nc.tensor.matmul(
-                    out=x[:, at : at + n].rearrange("p (n t) -> p n t", t=4), lhsT=identb[:], rhs=v, start=True, stop=True
-                )
-                at += n
-
-        def mv_il(key, src, lo, hi):
-            c = cols(lo, hi)
-            v = src[:].rearrange("p t n -> p n t")
-            mv(key, [v[:, a : min(a + P, c.stop), :] for a in range(c.start, c.stop, P)])
-
-        def mv_w(key, k, t0, t1):
-            v = wraw[k][:].rearrange("p j (m t) -> p t m j", t=4)
-            mv(key, [v[:, t] for t in range(t0, t1)])
-
-        def mc(eng, key, dst, lo, hi):
-            c = cols(lo, hi)
-            cp(eng, dst.rearrange("p n t -> p (n t)")[:, 4 * c.start : 4 * c.stop], bank["m", key][:, : 4 * (c.stop - c.start)])
 
         def quant(codes, scales, src, lo, hi, fmt):
             c = cols(lo, hi)
@@ -202,10 +178,9 @@ def tile_spatialgcn_pb_v_kernel(
         with tc.manual_schedule():
             nc.scalar.dma_start(out=gam[:], in_=gamma.rearrange("(p j) -> p j", j=4))
             nc.scalar.dma_start(out=rst[:], in_=rstd.rearrange("(p j) -> p j", j=4))
-            make_identity(nc, identb[:])
             make_identity(nc, ident[:])
-            for j in (0, 2):
-                ld(graw[0][:, j : j + 2, :], grad_out[0].rearrange(pj, j=4)[:, j : j + 2, :])
+            for j in range(4):
+                ld(graw[0][:, j, :], grad_out[0].rearrange(pj, j=4)[:, j, :])
             ld(wraw[1][:], wg[:, 1024:1536].rearrange(pj, j=4))
             ld(graw[1][:], grad_out[1].rearrange(pj, j=4))
             ld(araw[:], adp.rearrange(pj, j=4))
@@ -213,114 +188,77 @@ def tile_spatialgcn_pb_v_kernel(
             for b in range(B):
                 ld(xraw[b][:], x1[b].rearrange(pj, j=4))
             V.tensor_tensor(out=fac[:], in0=gam[:], in1=rst[:], op=MULT)
-            scale(0, 0)
-            scale(0, 1)
-            scale(0, 2)
-            scale(0, 3)
+            for j in range(4):
+                scale(0, j)
             il(V, dzi[0], dz[0], 0, 5)
-            il_w(V, 1, 0, 2)
-            scale(1, 0)
-            scale(1, 1)
             il(S, dzi[0], dz[0], 5, 8)
-            q_w(1, 0, 2)
-            scale(1, 2)
-            scale(1, 3)
             q_dz(0, 0, 8)
-            il_w(S, 1, 2, 4)
-            q_w(1, 2, 4)
-            il(S, ai, araw, 0, 4)
+            for t in (0, 2):
+                il_w(S, 1, t, t + 2)
+            for j in range(4):
+                scale(1, j)
+            q_w(1, 0, 2)
             d2(0, 0)
-            il(S, dzi[1], dz[1], 0, 4)
-            il(V, dzi[1], dz[1], 4, 8)
-            il(V, ai, araw, 4, 8)
-            q_dz(1, 0, 8)
             d2(0, 1)
-            evd(S, 0, 0)
-            evd(S, 0, 1)
-            il(V, xi[0], xraw[0], 0, 4)
+            il(V, dzi[1], dz[1], 0, 8)
+            q_w(1, 2, 4)
             d2(0, 2)
-            d2(1, 0)
-            evd(S, 0, 2)
-            evd(S, 1, 0)
-            d2(1, 1)
-            tr(0, 0)
-            il_w(V, 0, 0, 2)
-            evd(S, 1, 1)
             d2(0, 3)
-            d2(1, 2)
-            il_w(V, 0, 2, 4)
-            d2(1, 3)
-            q_a(0, 8)
-            wc(S, 0, 0)
-            q_t(0, 0, 2)
-            q_w(0, 0, 2)
-            evd(S, 0, 3)
-            evd(V, 1, 2)
-            il(V, xi[1], xraw[1], 0, 4)
-            tr(1, 0)
+            il(S, ai, araw, 0, 4)
+            q_dz(1, 0, 8)
+            for t in range(4):
+                evd(S, 0, t)
+            for t in range(4):
+                d2(1, t)
+            tr(0, 0)
             tr(0, 2)
+            il_w(V, 0, 0, 4)
+            il(V, ai, araw, 4, 8)
+            evd(S, 1, 0)
+            evd(V, 1, 1)
+            evd(S, 1, 2)
             evd(S, 1, 3)
-            wc(S, 1, 0)
+            tr(1, 0)
+            tr(1, 2)
+            q_a(0, 8)
+            il(V, xi[0], xraw[0], 0, 4)
+            q_w(0, 0, 4)
+            wc(S, 0, 0)
             wc(S, 0, 2)
+            q_t(0, 0, 2)
+            wc(S, 1, 0)
+            wc(S, 1, 2)
             d1(0, 0)
             hop(0, 0)
-            evo(S, 0, 0)
             d1(0, 1)
             hop(0, 1)
-            tr(1, 2)
-            evo(S, 0, 1)
-            q_t(1, 0, 2)
-            wc(S, 1, 2)
+            il(V, di[0], ev[0], 0, 8)
             q_t(0, 2, 4)
-            d1(1, 0)
-            hop(1, 0)
-            il(V, di[0], ev[0], 0, 4)
-            q_w(0, 2, 4)
-            il(V, di[1], ev[1], 0, 4)
-            evo(S, 1, 0)
-            st_o(0, 0, 2)
-            il(V, xi[1], xraw[1], 4, 8)
-            q_d(0, 0, 4)
-            d1(1, 1)
-            hop(1, 1)
-            d1(0, 2)
-            hop(0, 2)
-            evo(S, 1, 1)
+            q_t(1, 0, 4)
             il(S, xi[0], xraw[0], 4, 8)
-            st_o(1, 0, 2)
-            q_t(1, 2, 4)
-            d1(0, 3)
-            hop(0, 3)
-            q_d(1, 0, 4)
-            evo(S, 0, 2)
-            d1(1, 2)
-            hop(1, 2)
-            q_x(1, 0, 8)
-            evo(S, 0, 3)
+            for t in (2, 3):
+                d1(0, t)
+                hop(0, t)
+            for t in range(4):
+                evo(S, 0, t)
+                st_o(0, t, t + 1)
+            for t in range(4):
+                d1(1, t)
+                hop(1, t)
+            q_d(0, 0, 8)
+            il(V, di[1], ev[1], 0, 4)
+            il(V, xi[1], xraw[1], 0, 8)
             q_x(0, 0, 8)
-            d1(1, 3)
-            hop(1, 3)
-            dadp(0, 0)
-            dadp(0, 1)
-            dadp(1, 0)
-            st_o(0, 2, 4)
-            il(V, di[0], ev[0], 4, 8)
+            q_d(1, 0, 4)
+            for t in range(4):
+                evo(S, 1, t)
+                st_o(1, t, t + 1)
+            for i in range(4):
+                dadp(0, i)
+            q_x(1, 0, 8)
             il(V, di[1], ev[1], 4, 8)
-            q_d(0, 4, 8)
-            evo(S, 1, 2)
-            dadp(1, 1)
-            evo(S, 1, 3)
             q_d(1, 4, 8)
-            st_o(1, 2, 4)
-            dadp(0, 2)
-            eva(S, 0)
-            st_a(0)
-            dadp(1, 2)
-            eva(S, 1)
-            st_a(1)
-            dadp(0, 3)
-            eva(S, 2)
-            st_a(2)
-            dadp(1, 3)
-            eva(S, 3)
-            st_a(3)
+            for i in range(4):
+                dadp(1, i)
+                eva(S if i % 2 == 0 else V, i)
+                st_a(i)

@@ -3,8 +3,14 @@ from contextlib import ExitStack
 import concourse.mybir as mybir
 from concourse.masks import make_identity
 
-FLOPS = 2 * (2 * 512 * 1024 * 512) + 2 * 1024 * 512 * 512 + 2 * 512 * 1024 * 512
-BYTES = 2 * (2 * 512 * 512 + 512 * 1024 + 2 * 512 * 512 + 512 * 512 + 512) + 4 * 512 + 4 * (2 * 512 * 512 + 512 * 512)
+B = 2
+N = 512
+P = 128
+PACK = 4
+HALF = N // 2
+
+FLOPS = 2 * B * N * (2 * N) * N + 2 * B * N * N * N + 2 * N * (B * N) * N
+BYTES = 2 * (B * N * N + N * 2 * N + B * N * N + N * N + N) + 4 * (N + B * N * N + N * N)
 
 F32 = mybir.dt.float32
 BF16 = mybir.dt.bfloat16
@@ -14,251 +20,245 @@ E4M3 = mybir.dt.float8_e4m3fn_x4
 E5M2 = mybir.dt.float8_e5m2_x4
 MULT = mybir.AluOpType.mult
 
-P = 128
-N = 512
-B = 2
+FIRST_SPLIT = 320
 
 
 def tile_spatialgcn_pb_v_kernel(
     tc, h, x1, adp, wg, bg, gamma, beta, rmean, rvar, rstd, grad_out, out_0, out_1
 ):
     nc = tc.nc
+    vector, scalar = nc.vector, nc.scalar
+
     with ExitStack() as ctx:
-        sb = ctx.enter_context(tc.tile_pool(name="sb", bufs=1))
-        ps = ctx.enter_context(tc.psum_pool(name="ps", bufs=1))
+        sbuf = ctx.enter_context(tc.tile_pool(name="sbuf", bufs=1))
+        psum = ctx.enter_context(tc.psum_pool(name="psum", bufs=1))
 
-        def tile(name, shape, dtype):
-            return sb.tile([P] + shape, dtype, name=name, align_bytes=256)
+        def sbuf_tile(name, shape, dtype):
+            return sbuf.tile([P] + shape, dtype, name=name, align_bytes=256)
 
-        gam = tile("gam", [4], BF16)
-        rst = tile("rst", [4], F32)
-        fac = tile("fac", [4], F32)
-        ident = tile("ident", [P], F32)
-        graw = [tile("graw%d" % b, [4, N], BF16) for b in range(B)]
-        dz = [tile("dz%d" % b, [4, N], BF16) for b in range(B)]
-        dzi = [tile("dzi%d" % b, [N, 4], BF16) for b in range(B)]
-        dzq = [tile("dzq%d" % b, [N], U32) for b in range(B)]
-        dzs = [tile("dzs%d" % b, [N], U8) for b in range(B)]
-        wraw = [tile("wraw%d" % k, [4, N], BF16) for k in range(2)]
-        wi = [tile("wi%d" % k, [4, P, 4], BF16) for k in range(2)]
-        wq = [tile("wq%d" % k, [N], U32) for k in range(2)]
-        ws = [tile("ws%d" % k, [N], U8) for k in range(2)]
-        xraw = [tile("xraw%d" % b, [4, N], BF16) for b in range(B)]
-        xi = [tile("xi%d" % b, [N, 4], BF16) for b in range(B)]
-        xq = [tile("xq%d" % b, [N], U32) for b in range(B)]
-        xs = [tile("xs%d" % b, [N], U8) for b in range(B)]
-        araw = tile("araw", [4, N], BF16)
-        ai = tile("ai", [N, 4], BF16)
-        aq = tile("aq", [N], U32)
-        asc = tile("asc", [N], U8)
-        ev = [tile("ev%d" % b, [4, N], BF16) for b in range(B)]
-        di = [tile("di%d" % b, [N, 4], BF16) for b in range(B)]
-        dq = [tile("dq%d" % b, [N], U32) for b in range(B)]
-        ds = [tile("ds%d" % b, [N], U8) for b in range(B)]
-        ti = [tile("ti%d" % b, [4, P, 4], BF16) for b in range(B)]
-        tq = [tile("tq%d" % b, [N], U32) for b in range(B)]
-        ts = [tile("ts%d" % b, [N], U8) for b in range(B)]
-        o0 = [tile("o0_%d" % b, [4, N], F32) for b in range(B)]
-        o1 = tile("o1", [4, N], F32)
+        def rows_tile(name):
+            return sbuf_tile(name, [PACK, N], BF16)
 
-        V, S = nc.vector, nc.scalar
-        nbank = [0]
-        bank = {}
+        def operand(name, fmt):
+            packed = sbuf_tile(name + "_packed", [N, PACK], BF16)
+            codes = sbuf_tile(name + "_codes", [N], U32)
+            scales = sbuf_tile(name + "_scales", [N], U8)
+            return packed, codes, scales, fmt
 
-        def alloc(key, shape=(N,), dtype=F32):
-            k = nbank[0] % 8
-            nbank[0] += 1
-            bank[key] = ps.tile([P] + list(shape), dtype, name="pb%d" % k, tag="pb%d" % k)
-            return bank[key]
+        gamma_col = sbuf_tile("gamma_col", [PACK], BF16)
+        rstd_col = sbuf_tile("rstd_col", [PACK], F32)
+        factor = sbuf_tile("factor", [PACK], F32)
+        identity = sbuf_tile("identity", [P], F32)
 
-        def cp(eng, out, in_):
-            if eng is nc.scalar:
-                eng.copy(out=out, in_=in_)
+        grad_rows = [rows_tile("grad_rows%d" % b) for b in range(B)]
+        dz2_rows = [rows_tile("dz2_rows%d" % b) for b in range(B)]
+        w_d1_rows = rows_tile("w_d1_rows")
+        w_d2_rows = rows_tile("w_d2_rows")
+        adp_rows = rows_tile("adp_rows")
+        x1_rows = [rows_tile("x1_rows%d" % b) for b in range(B)]
+        d2_rows = [rows_tile("d2_rows%d" % b) for b in range(B)]
+
+        dz2 = [operand("dz2_%d" % b, E5M2) for b in range(B)]
+        w_d1 = operand("w_d1", E4M3)
+        w_d2 = operand("w_d2", E4M3)
+        d2_w = [operand("d2_w%d" % b, E5M2) for b in range(B)]
+        d2_c = [operand("d2_c%d" % b, E5M2) for b in range(B)]
+        adp_op = operand("adp", E4M3)
+        x1_op = [operand("x1_%d" % b, E4M3) for b in range(B)]
+
+        out_0_rows = [sbuf_tile("out_0_rows%d" % b, [PACK, N], F32) for b in range(B)]
+        out_1_rows = sbuf_tile("out_1_rows", [N // P, N], F32)
+
+        def load(tile, rows):
+            nc.sync.dma_start(out=tile[:], in_=rows.rearrange("(p j) n -> p j n", j=PACK))
+
+        def copy(engine, out, in_):
+            if engine is scalar:
+                scalar.copy(out=out, in_=in_)
             else:
-                eng.tensor_copy(out=out, in_=in_)
+                vector.tensor_copy(out=out, in_=in_)
 
-        def scale(b, j):
-            V.tensor_scalar(out=dz[b][:, j, :], in0=graw[b][:, j, :], scalar1=fac[:, j : j + 1], scalar2=None, op0=MULT)
+        def scale_grad(b):
+            for j in range(PACK):
+                vector.tensor_scalar(
+                    out=dz2_rows[b][:, j, :],
+                    in0=grad_rows[b][:, j, :],
+                    scalar1=factor[:, j : j + 1],
+                    scalar2=None,
+                    op0=MULT,
+                )
 
-        def cols(lo, hi):
-            return slice(lo * N // 8, hi * N // 8)
-
-        def il(eng, dst, src, lo, hi):
-            c = cols(lo, hi)
-            cp(eng, dst[:, c, :].rearrange("p (n i) t -> p n t i", i=4), src[:, :, c].rearrange("p t (n i) -> p n t i", i=4))
-
-        def il_w(eng, k, t0, t1):
-            cp(eng, wi[k][:, t0:t1], wraw[k][:].rearrange("p j (m t) -> p t m j", t=4)[:, t0:t1])
-
-        def quant(codes, scales, src, lo, hi, fmt):
-            c = cols(lo, hi)
-            V.quantize_mx(
-                out=codes[:, c].bitcast(fmt),
-                scales=scales[:, c],
-                in_=src.rearrange("p n t -> p (n t)")[:, 4 * c.start : 4 * c.stop],
+        def interleave(engine, op, rows, first, last):
+            copy(
+                engine,
+                op[0][:, first:last, :].rearrange("p (n i) j -> p n j i", i=4),
+                rows[:, :, first:last].rearrange("p j (n i) -> p n j i", i=4),
             )
 
-        def q_dz(b, lo, hi):
-            quant(dzq[b], dzs[b], dzi[b][:], lo, hi, E5M2)
+        def interleave_weight(engine, op, rows, t0, t1):
+            copy(
+                engine,
+                op[0][:, P * t0 : P * t1, :].rearrange("p (t m) j -> p t m j", m=P),
+                rows[:].rearrange("p j (m t) -> p t m j", t=4)[:, t0:t1],
+            )
 
-        def q_w(k, t0, t1):
-            quant(wq[k], ws[k], wi[k][:].rearrange("p t m j -> p (t m) j"), 2 * t0, 2 * t1, E4M3)
+        def quantize(op, first, last):
+            packed, codes, scales, fmt = op
+            vector.quantize_mx(
+                out=codes[:, first:last].bitcast(fmt),
+                scales=scales[:, first:last],
+                in_=packed[:].rearrange("p n j -> p (n j)")[:, PACK * first : PACK * last],
+            )
 
-        def q_x(b, lo, hi):
-            quant(xq[b], xs[b], xi[b][:], lo, hi, E4M3)
-
-        def q_a(lo, hi):
-            quant(aq, asc, ai[:], lo, hi, E4M3)
-
-        def q_d(b, lo, hi):
-            quant(dq[b], ds[b], di[b][:], lo, hi, E5M2)
-
-        def q_t(b, t0, t1):
-            quant(tq[b], ts[b], ti[b][:].rearrange("p t c e -> p (t c) e"), 2 * t0, 2 * t1, E5M2)
-
-        def mx(out, l, ls, lf, i, r, rs, rf, start, stop):
-            m = slice(P * i, P * i + P)
+        def mx_pass(out, stationary, block, moving, start, stop):
+            m = slice(P * block, P * block + P)
             nc.tensor.matmul_mx(
                 out=out[:],
-                lhsT=l[:, m].bitcast(lf),
-                lhsT_scale=ls[:, m],
-                rhs=r[:].bitcast(rf),
-                rhs_scale=rs[:],
+                lhsT=stationary[1][:, m].bitcast(stationary[3]),
+                lhsT_scale=stationary[2][:, m],
+                rhs=moving[1][:].bitcast(moving[3]),
+                rhs_scale=moving[2][:],
                 start=start,
                 stop=stop,
             )
 
-        def d2(b, t):
-            mx(alloc(("d", b, t)), wq[1], ws[1], E4M3, t, dzq[b], dzs[b], E5M2, True, True)
+        def bank(k, shape):
+            return psum.tile([P] + shape, F32, name="bank%d" % k, tag="bank%d" % k)
 
-        def evd(eng, b, t):
-            cp(eng, ev[b][:, t, :], bank["d", b, t][:])
+        d2_sum, transposed, out_0_sum, out_1_sum = {}, {}, {}, {}
 
-        def tr(b, t0):
-            x = alloc(("x", b, t0), (2, 2, P))
-            for t in range(2):
-                w = ev[b][:, t0 + t, :].bitcast(F32)
+        def multiply_d2(b, t):
+            d2_sum[b, t] = bank(4 * b + t, [N])
+            mx_pass(d2_sum[b, t], w_d2, t, dz2[b], True, True)
+
+        def empty_d2(engine, b, t):
+            copy(engine, d2_rows[b][:, t, :], d2_sum[b, t][:])
+
+        def transpose_d2(b, t0):
+            transposed[b, t0] = bank(2 * b + t0 // 2, [2, 2, P])
+            for i in range(2):
+                words = d2_rows[b][:, t0 + i, :].bitcast(F32)
                 for u in range(2):
-                    nc.tensor.transpose(x[:, t, u, :], w[:, u::2], ident[:])
+                    nc.tensor.transpose(transposed[b, t0][:, i, u, :], words[:, u::2], identity[:])
 
-        def wc(eng, b, t0):
-            cp(
-                eng,
-                ti[b][:, t0 : t0 + 2].rearrange("p t c e -> p t (c e)").bitcast(F32).rearrange("p t (c u) -> p t c u", u=2),
-                bank["x", b, t0][:].rearrange("p t u c -> p t c u"),
+        def empty_transposed(engine, b, t0):
+            packed = d2_w[b][0][:, P * t0 : P * (t0 + 2), :].rearrange("p c e -> p (c e)")
+            copy(
+                engine,
+                packed.bitcast(F32).rearrange("p (i m u) -> p i m u", i=2, u=2),
+                transposed[b, t0][:].rearrange("p i u m -> p i m u"),
             )
 
-        def d1(b, t):
-            mx(alloc(("o", b, t)), wq[0], ws[0], E4M3, t, dzq[b], dzs[b], E5M2, True, False)
+        def start_out_0(b, t):
+            out_0_sum[b, t] = bank(4 * (1 - b) + t, [N])
+            mx_pass(out_0_sum[b, t], w_d1, t, dz2[b], True, False)
 
-        def hop(b, t):
-            mx(bank["o", b, t], tq[b], ts[b], E5M2, t, aq, asc, E4M3, False, True)
+        def finish_out_0(b, t):
+            mx_pass(out_0_sum[b, t], d2_w[b], t, adp_op, False, True)
 
-        def dadp(b, i):
+        def store_out_0(b, t):
+            copy(scalar, out_0_rows[b][:, t, :], out_0_sum[b, t][:])
+            nc.sync.dma_start(
+                out=out_0[b].rearrange("(p t) v -> p t v", t=4)[:, t, :],
+                in_=out_0_rows[b][:, t, :],
+            )
+
+        def multiply_out_1(b, i):
             if b == 0:
-                alloc(("a", i))
-            mx(bank["a", i], dq[b], ds[b], E5M2, i, xq[b], xs[b], E4M3, b == 0, b == B - 1)
+                out_1_sum[i] = bank(4 + i, [N])
+            mx_pass(out_1_sum[i], d2_c[b], i, x1_op[b], b == 0, b == B - 1)
 
-        def evo(eng, b, t):
-            cp(eng, o0[b][:, t, :], bank["o", b, t][:])
+        def store_out_1(engine, i):
+            copy(engine, out_1_rows[:, i, :], out_1_sum[i][:])
+            nc.sync.dma_start(out=out_1[P * i : P * i + P, :], in_=out_1_rows[:, i, :])
 
-        def eva(eng, i):
-            cp(eng, o1[:, i, :], bank["a", i][:])
-
-        def st_o(b, t0, t1):
-            nc.sync.dma_start(out=out_0[b].rearrange("(p t) v -> p t v", t=4)[:, t0:t1, :], in_=o0[b][:, t0:t1, :])
-
-        def st_a(i):
-            nc.sync.dma_start(out=out_1[P * i : P * i + P, :], in_=o1[:, i, :])
-
-        def ld(dst, src):
-            nc.sync.dma_start(out=dst, in_=src)
-
-        pj = "(p j) n -> p j n"
         with tc.manual_schedule():
-            nc.scalar.dma_start(out=gam[:], in_=gamma.rearrange("(p j) -> p j", j=4))
-            nc.scalar.dma_start(out=rst[:], in_=rstd.rearrange("(p j) -> p j", j=4))
-            make_identity(nc, ident[:])
-            for j in range(4):
-                ld(graw[0][:, j, :], grad_out[0].rearrange(pj, j=4)[:, j, :])
-            ld(wraw[1][:], wg[:, 1024:1536].rearrange(pj, j=4))
-            ld(graw[1][:], grad_out[1].rearrange(pj, j=4))
-            ld(araw[:], adp.rearrange(pj, j=4))
-            ld(wraw[0][:], wg[:, 512:1024].rearrange(pj, j=4))
+            nc.scalar.dma_start(out=gamma_col[:], in_=gamma.rearrange("(p j) -> p j", j=PACK))
+            nc.scalar.dma_start(out=rstd_col[:], in_=rstd.rearrange("(p j) -> p j", j=PACK))
+            make_identity(nc, identity[:])
+
+            for j in range(PACK):
+                nc.sync.dma_start(
+                    out=grad_rows[0][:, j, :],
+                    in_=grad_out[0].rearrange("(p j) n -> p j n", j=PACK)[:, j, :],
+                )
+            load(w_d2_rows, wg[:, 2 * N : 3 * N])
+            load(grad_rows[1], grad_out[1])
+            load(adp_rows, adp)
+            load(w_d1_rows, wg[:, N : 2 * N])
             for b in range(B):
-                ld(xraw[b][:], x1[b].rearrange(pj, j=4))
-            V.tensor_tensor(out=fac[:], in0=gam[:], in1=rst[:], op=MULT)
-            for j in range(4):
-                scale(0, j)
-            il(V, dzi[0], dz[0], 0, 5)
-            il(S, dzi[0], dz[0], 5, 8)
-            q_dz(0, 0, 8)
-            for t in (0, 2):
-                il_w(S, 1, t, t + 2)
-            for j in range(4):
-                scale(1, j)
-            q_w(1, 0, 2)
-            d2(0, 0)
-            d2(0, 1)
-            il(V, dzi[1], dz[1], 0, 8)
-            q_w(1, 2, 4)
-            d2(0, 2)
-            d2(0, 3)
-            il(S, ai, araw, 0, 4)
-            q_dz(1, 0, 8)
+                load(x1_rows[b], x1[b])
+
+            vector.tensor_tensor(out=factor[:], in0=gamma_col[:], in1=rstd_col[:], op=MULT)
+            scale_grad(0)
+            interleave(vector, dz2[0], dz2_rows[0], 0, FIRST_SPLIT)
+            interleave(scalar, dz2[0], dz2_rows[0], FIRST_SPLIT, N)
+            quantize(dz2[0], 0, N)
+            interleave_weight(scalar, w_d2, w_d2_rows, 0, 2)
+            interleave_weight(scalar, w_d2, w_d2_rows, 2, 4)
+            scale_grad(1)
+            quantize(w_d2, 0, HALF)
+            multiply_d2(0, 0)
+            multiply_d2(0, 1)
+            interleave(vector, dz2[1], dz2_rows[1], 0, N)
+            quantize(w_d2, HALF, N)
+            multiply_d2(0, 2)
+            multiply_d2(0, 3)
+            interleave(scalar, adp_op, adp_rows, 0, HALF)
+            quantize(dz2[1], 0, N)
             for t in range(4):
-                evd(S, 0, t)
+                empty_d2(scalar, 0, t)
             for t in range(4):
-                d2(1, t)
-            tr(0, 0)
-            tr(0, 2)
-            il_w(V, 0, 0, 4)
-            il(V, ai, araw, 4, 8)
-            evd(S, 1, 0)
-            evd(V, 1, 1)
-            evd(S, 1, 2)
-            evd(S, 1, 3)
-            tr(1, 0)
-            tr(1, 2)
-            q_a(0, 8)
-            il(V, xi[0], xraw[0], 0, 4)
-            q_w(0, 0, 4)
-            wc(S, 0, 0)
-            wc(S, 0, 2)
-            q_t(0, 0, 2)
-            wc(S, 1, 0)
-            wc(S, 1, 2)
-            d1(0, 0)
-            hop(0, 0)
-            d1(0, 1)
-            hop(0, 1)
-            il(V, di[0], ev[0], 0, 8)
-            q_t(0, 2, 4)
-            q_t(1, 0, 4)
-            il(S, xi[0], xraw[0], 4, 8)
+                multiply_d2(1, t)
+
+            transpose_d2(0, 0)
+            transpose_d2(0, 2)
+            interleave_weight(vector, w_d1, w_d1_rows, 0, 4)
+            interleave(vector, adp_op, adp_rows, HALF, N)
+            for t in range(4):
+                empty_d2(vector if t == 1 else scalar, 1, t)
+            transpose_d2(1, 0)
+            transpose_d2(1, 2)
+            quantize(adp_op, 0, N)
+            quantize(w_d1, 0, N)
+            interleave(vector, x1_op[0], x1_rows[0], 0, HALF)
+            empty_transposed(scalar, 0, 0)
+            empty_transposed(scalar, 0, 2)
+            quantize(d2_w[0], 0, HALF)
+            empty_transposed(scalar, 1, 0)
+            empty_transposed(scalar, 1, 2)
+            start_out_0(0, 0)
+            start_out_0(0, 1)
+            finish_out_0(0, 0)
+            finish_out_0(0, 1)
+            interleave(vector, d2_c[0], d2_rows[0], 0, N)
+            quantize(d2_w[0], HALF, N)
+            quantize(d2_w[1], 0, N)
+
+            store_out_0(0, 0)
+            store_out_0(0, 1)
+            interleave(scalar, x1_op[0], x1_rows[0], HALF, N)
             for t in (2, 3):
-                d1(0, t)
-                hop(0, t)
+                start_out_0(0, t)
+                finish_out_0(0, t)
+            store_out_0(0, 2)
+            store_out_0(0, 3)
             for t in range(4):
-                evo(S, 0, t)
-                st_o(0, t, t + 1)
+                start_out_0(1, t)
+                finish_out_0(1, t)
+            quantize(d2_c[0], 0, N)
+            interleave(vector, d2_c[1], d2_rows[1], 0, HALF)
+            interleave(vector, x1_op[1], x1_rows[1], 0, N)
+            quantize(x1_op[0], 0, N)
+            quantize(d2_c[1], 0, HALF)
             for t in range(4):
-                d1(1, t)
-                hop(1, t)
-            q_d(0, 0, 8)
-            il(V, di[1], ev[1], 0, 4)
-            il(V, xi[1], xraw[1], 0, 8)
-            q_x(0, 0, 8)
-            q_d(1, 0, 4)
-            for t in range(4):
-                evo(S, 1, t)
-                st_o(1, t, t + 1)
+                store_out_0(1, t)
+
             for i in range(4):
-                dadp(0, i)
-            q_x(1, 0, 8)
-            il(V, di[1], ev[1], 4, 8)
-            q_d(1, 4, 8)
+                multiply_out_1(0, i)
+            quantize(x1_op[1], 0, N)
+            interleave(vector, d2_c[1], d2_rows[1], HALF, N)
+            quantize(d2_c[1], HALF, N)
             for i in range(4):
-                dadp(1, i)
-                eva(S if i % 2 == 0 else V, i)
-                st_a(i)
+                multiply_out_1(1, i)
+                store_out_1(scalar if i % 2 == 0 else vector, i)

@@ -91,8 +91,8 @@ def tile_spatialgcn_pb_v_kernel(
         def interleave(engine, op, rows, first, last):
             copy(
                 engine,
-                op[0][:, first:last, :].rearrange("p (n i) j -> p n j i", i=4),
-                rows[:, :, first:last].rearrange("p j (n i) -> p n j i", i=4),
+                op[0][:, first:last, :].rearrange("p (n i) j -> p n j i", i=8),
+                rows[:, :, first:last].rearrange("p j (n i) -> p n j i", i=8),
             )
 
         def interleave_weight(engine, op, rows, t0, t1):

from contextlib import ExitStack

import concourse.mybir as mybir
from concourse.masks import make_identity

B = 2
N = 512
P = 128
PACK = 4
HALF = N // 2

FLOPS = 2 * B * N * (2 * N) * N + 2 * B * N * N * N + 2 * N * (B * N) * N
BYTES = 2 * (B * N * N + N * 2 * N + B * N * N + N * N + N) + 4 * (N + B * N * N + N * N)

F32 = mybir.dt.float32
BF16 = mybir.dt.bfloat16
U32 = mybir.dt.uint32
U8 = mybir.dt.uint8
E4M3 = mybir.dt.float8_e4m3fn_x4
E5M2 = mybir.dt.float8_e5m2_x4
MULT = mybir.AluOpType.mult

FIRST_SPLIT = 320


def tile_spatialgcn_pb_v_kernel(
    tc, h, x1, adp, wg, bg, gamma, beta, rmean, rvar, rstd, grad_out, out_0, out_1
):
    nc = tc.nc
    vector, scalar = nc.vector, nc.scalar

    with ExitStack() as ctx:
        sbuf = ctx.enter_context(tc.tile_pool(name="sbuf", bufs=1))
        psum = ctx.enter_context(tc.psum_pool(name="psum", bufs=1))

        def sbuf_tile(name, shape, dtype):
            return sbuf.tile([P] + shape, dtype, name=name, align_bytes=256)

        def rows_tile(name):
            return sbuf_tile(name, [PACK, N], BF16)

        def operand(name, fmt):
            packed = sbuf_tile(name + "_packed", [N, PACK], BF16)
            codes = sbuf_tile(name + "_codes", [N], U32)
            scales = sbuf_tile(name + "_scales", [N], U8)
            return packed, codes, scales, fmt

        gamma_col = sbuf_tile("gamma_col", [PACK], BF16)
        rstd_col = sbuf_tile("rstd_col", [PACK], F32)
        factor = sbuf_tile("factor", [PACK], F32)
        identity = sbuf_tile("identity", [P], F32)

        grad_rows = [rows_tile("grad_rows%d" % b) for b in range(B)]
        dz2_rows = [rows_tile("dz2_rows%d" % b) for b in range(B)]
        w_d1_rows = rows_tile("w_d1_rows")
        w_d2_rows = rows_tile("w_d2_rows")
        adp_rows = rows_tile("adp_rows")
        x1_rows = [rows_tile("x1_rows%d" % b) for b in range(B)]
        d2_rows = [rows_tile("d2_rows%d" % b) for b in range(B)]

        dz2 = [operand("dz2_%d" % b, E5M2) for b in range(B)]
        w_d1 = operand("w_d1", E4M3)
        w_d2 = operand("w_d2", E4M3)
        d2_w = [operand("d2_w%d" % b, E5M2) for b in range(B)]
        d2_c = [operand("d2_c%d" % b, E5M2) for b in range(B)]
        adp_op = operand("adp", E4M3)
        x1_op = [operand("x1_%d" % b, E4M3) for b in range(B)]

        out_0_rows = [sbuf_tile("out_0_rows%d" % b, [PACK, N], F32) for b in range(B)]
        out_1_rows = sbuf_tile("out_1_rows", [N // P, N], F32)

        def load(tile, rows):
            nc.sync.dma_start(out=tile[:], in_=rows.rearrange("(p j) n -> p j n", j=PACK))

        def copy(engine, out, in_):
            if engine is scalar:
                scalar.copy(out=out, in_=in_)
            else:
                vector.tensor_copy(out=out, in_=in_)

        def scale_grad(b):
            for j in range(PACK):
                vector.tensor_scalar(
                    out=dz2_rows[b][:, j, :],
                    in0=grad_rows[b][:, j, :],
                    scalar1=factor[:, j : j + 1],
                    scalar2=None,
                    op0=MULT,
                )

        def interleave(engine, op, rows, first, last):
            copy(
                engine,
                op[0][:, first:last, :].rearrange("p (n i) j -> p n j i", i=8),
                rows[:, :, first:last].rearrange("p j (n i) -> p n j i", i=8),
            )

        def interleave_weight(engine, op, rows, t0, t1):
            copy(
                engine,
                op[0][:, P * t0 : P * t1, :].rearrange("p (t m) j -> p t m j", m=P),
                rows[:].rearrange("p j (m t) -> p t m j", t=4)[:, t0:t1],
            )

        def quantize(op, first, last):
            packed, codes, scales, fmt = op
            vector.quantize_mx(
                out=codes[:, first:last].bitcast(fmt),
                scales=scales[:, first:last],
                in_=packed[:].rearrange("p n j -> p (n j)")[:, PACK * first : PACK * last],
            )

        def mx_pass(out, stationary, block, moving, start, stop):
            m = slice(P * block, P * block + P)
            nc.tensor.matmul_mx(
                out=out[:],
                lhsT=stationary[1][:, m].bitcast(stationary[3]),
                lhsT_scale=stationary[2][:, m],
                rhs=moving[1][:].bitcast(moving[3]),
                rhs_scale=moving[2][:],
                start=start,
                stop=stop,
            )

        def bank(k, shape):
            return psum.tile([P] + shape, F32, name="bank%d" % k, tag="bank%d" % k)

        d2_sum, transposed, out_0_sum, out_1_sum = {}, {}, {}, {}

        def multiply_d2(b, t):
            d2_sum[b, t] = bank(4 * b + t, [N])
            mx_pass(d2_sum[b, t], w_d2, t, dz2[b], True, True)

        def empty_d2(engine, b, t):
            copy(engine, d2_rows[b][:, t, :], d2_sum[b, t][:])

        def transpose_d2(b, t0):
            transposed[b, t0] = bank(2 * b + t0 // 2, [2, 2, P])
            for i in range(2):
                words = d2_rows[b][:, t0 + i, :].bitcast(F32)
                for u in range(2):
                    nc.tensor.transpose(transposed[b, t0][:, i, u, :], words[:, u::2], identity[:])

        def empty_transposed(engine, b, t0):
            packed = d2_w[b][0][:, P * t0 : P * (t0 + 2), :].rearrange("p c e -> p (c e)")
            copy(
                engine,
                packed.bitcast(F32).rearrange("p (i m u) -> p i m u", i=2, u=2),
                transposed[b, t0][:].rearrange("p i u m -> p i m u"),
            )

        def start_out_0(b, t):
            out_0_sum[b, t] = bank(4 * (1 - b) + t, [N])
            mx_pass(out_0_sum[b, t], w_d1, t, dz2[b], True, False)

        def finish_out_0(b, t):
            mx_pass(out_0_sum[b, t], d2_w[b], t, adp_op, False, True)

        def store_out_0(b, t):
            copy(scalar, out_0_rows[b][:, t, :], out_0_sum[b, t][:])
            nc.sync.dma_start(
                out=out_0[b].rearrange("(p t) v -> p t v", t=4)[:, t, :],
                in_=out_0_rows[b][:, t, :],
            )

        def multiply_out_1(b, i):
            if b == 0:
                out_1_sum[i] = bank(4 + i, [N])
            mx_pass(out_1_sum[i], d2_c[b], i, x1_op[b], b == 0, b == B - 1)

        def store_out_1(engine, i):
            copy(engine, out_1_rows[:, i, :], out_1_sum[i][:])
            nc.sync.dma_start(out=out_1[P * i : P * i + P, :], in_=out_1_rows[:, i, :])

        with tc.manual_schedule():
            nc.scalar.dma_start(out=gamma_col[:], in_=gamma.rearrange("(p j) -> p j", j=PACK))
            nc.scalar.dma_start(out=rstd_col[:], in_=rstd.rearrange("(p j) -> p j", j=PACK))
            make_identity(nc, identity[:])

            for j in range(PACK):
                nc.sync.dma_start(
                    out=grad_rows[0][:, j, :],
                    in_=grad_out[0].rearrange("(p j) n -> p j n", j=PACK)[:, j, :],
                )
            load(w_d2_rows, wg[:, 2 * N : 3 * N])
            load(grad_rows[1], grad_out[1])
            load(adp_rows, adp)
            load(w_d1_rows, wg[:, N : 2 * N])
            for b in range(B):
                load(x1_rows[b], x1[b])

            vector.tensor_tensor(out=factor[:], in0=gamma_col[:], in1=rstd_col[:], op=MULT)
            scale_grad(0)
            interleave(vector, dz2[0], dz2_rows[0], 0, FIRST_SPLIT)
            interleave(scalar, dz2[0], dz2_rows[0], FIRST_SPLIT, N)
            quantize(dz2[0], 0, N)
            interleave_weight(scalar, w_d2, w_d2_rows, 0, 2)
            interleave_weight(scalar, w_d2, w_d2_rows, 2, 4)
            scale_grad(1)
            quantize(w_d2, 0, HALF)
            multiply_d2(0, 0)
            multiply_d2(0, 1)
            interleave(vector, dz2[1], dz2_rows[1], 0, N)
            quantize(w_d2, HALF, N)
            multiply_d2(0, 2)
            multiply_d2(0, 3)
            interleave(scalar, adp_op, adp_rows, 0, HALF)
            quantize(dz2[1], 0, N)
            for t in range(4):
                empty_d2(scalar, 0, t)
            for t in range(4):
                multiply_d2(1, t)

            transpose_d2(0, 0)
            transpose_d2(0, 2)
            interleave_weight(vector, w_d1, w_d1_rows, 0, 4)
            interleave(vector, adp_op, adp_rows, HALF, N)
            for t in range(4):
                empty_d2(vector if t == 1 else scalar, 1, t)
            transpose_d2(1, 0)
            transpose_d2(1, 2)
            quantize(adp_op, 0, N)
            quantize(w_d1, 0, N)
            interleave(vector, x1_op[0], x1_rows[0], 0, HALF)
            empty_transposed(scalar, 0, 0)
            empty_transposed(scalar, 0, 2)
            quantize(d2_w[0], 0, HALF)
            empty_transposed(scalar, 1, 0)
            empty_transposed(scalar, 1, 2)
            start_out_0(0, 0)
            start_out_0(0, 1)
            finish_out_0(0, 0)
            finish_out_0(0, 1)
            interleave(vector, d2_c[0], d2_rows[0], 0, N)
            quantize(d2_w[0], HALF, N)
            quantize(d2_w[1], 0, N)

            store_out_0(0, 0)
            store_out_0(0, 1)
            interleave(scalar, x1_op[0], x1_rows[0], HALF, N)
            for t in (2, 3):
                start_out_0(0, t)
                finish_out_0(0, t)
            store_out_0(0, 2)
            store_out_0(0, 3)
            for t in range(4):
                start_out_0(1, t)
                finish_out_0(1, t)
            quantize(d2_c[0], 0, N)
            interleave(vector, d2_c[1], d2_rows[1], 0, HALF)
            interleave(vector, x1_op[1], x1_rows[1], 0, N)
            quantize(x1_op[0], 0, N)
            quantize(d2_c[1], 0, HALF)
            for t in range(4):
                store_out_0(1, t)

            for i in range(4):
                multiply_out_1(0, i)
            quantize(x1_op[1], 0, N)
            interleave(vector, d2_c[1], d2_rows[1], HALF, N)
            quantize(d2_c[1], HALF, N)
            for i in range(4):
                multiply_out_1(1, i)
                store_out_1(scalar if i % 2 == 0 else vector, i)
